import numpy as np
import ml_dtypes


def mxq(x, axis, fmt="e4m3"):
    dtype, down = {"e4m3": (ml_dtypes.float8_e4m3fn, 7), "e5m2": (ml_dtypes.float8_e5m2, 14)}[fmt]
    v = np.moveaxis(np.asarray(x, np.float32).astype(ml_dtypes.bfloat16).astype(np.float64), axis, -1)
    blocks = v.reshape(v.shape[:-1] + (-1, 32))
    amax = np.abs(blocks).max(-1, keepdims=True)
    byte = np.maximum(np.where(amax > 0, np.frexp(amax)[1] - 1 + 127, 0) - down, 1)
    scale = np.exp2(byte - 127.0)
    codes = (blocks / scale).astype(np.float32).astype(dtype).astype(np.float64)
    return np.moveaxis((codes * scale).reshape(v.shape), -1, axis)


WIDE = False


def mx_kscale(k):
    if not WIDE:
        return np.ones(k)
    levels = np.array([10, -10, 5, -5, 0])
    a = np.random.permutation(np.resize(levels, k // 512 * 4)).reshape(k // 512, 4)
    idx = np.arange(k)
    return np.exp2(a[idx // 512, idx % 128 // 32])


BF16 = ml_dtypes.bfloat16


def bf(x):
    return np.asarray(x, np.float32).astype(BF16)


def f64(x):
    return np.asarray(x).astype(np.float64)


E2M1 = np.array([0.0, 0.5, 1.0, 1.5, 2.0, 3.0, 4.0, 6.0, -0.0, -0.5, -1.0, -1.5, -2.0, -3.0, -4.0, -6.0])


def pack_weight(w, fmt):
    k, n = w.shape
    w = f64(bf(w)).reshape(k // 32, 32, n)
    amax = np.abs(w).max(1)
    if fmt == "e4m3":
        byte = np.frexp(amax)[1] - 1 + 127 - 7
    else:
        mant, ex = np.frexp(amax / 6.0)
        byte = np.where(mant > 0.5, ex, ex - 1) + 127
    byte = np.clip(np.where(amax > 0, byte, 1), 1, 254)
    scaled = (w * np.exp2(127.0 - byte)[:, None, :]).reshape(k, n).astype(np.float32)
    by_word = np.ascontiguousarray(scaled.reshape(k // 512, 128, 4, n).transpose(0, 1, 3, 2))
    if fmt == "e4m3":
        words = by_word.astype(ml_dtypes.float8_e4m3fn).view(np.uint8)
    else:
        c = by_word.astype(ml_dtypes.float4_e2m1fn).view(np.uint8) & 0xF
        words = c[..., 0::2] | (c[..., 1::2] << 4)
    return np.ascontiguousarray(words), np.ascontiguousarray(byte.astype(np.uint8).reshape(k // 512, 16, n))


def unpack_weight(words, scales, fmt):
    g, p, n, _ = words.shape
    if fmt == "e4m3":
        vals = np.ascontiguousarray(words).view(ml_dtypes.float8_e4m3fn).astype(np.float64)
    else:
        nib = np.empty((g, p, n, 4), np.uint8)
        nib[..., 0::2] = words & 0xF
        nib[..., 1::2] = words >> 4
        vals = E2M1[nib]
    vals = vals * np.repeat(np.exp2(scales.astype(np.float64) - 127.0), 8, axis=1)[..., None]
    return vals.transpose(0, 1, 3, 2).reshape(g * 512, n)


BATCH, SEQ, IN_F, OUT_F, GRID_SIZE = 1, 128, 2048, 2048, 4
GRID_LO, GRID_HI = -2.0, 2.0


def _grid_and_inv_denom():
    grid = np.linspace(GRID_LO, GRID_HI, GRID_SIZE)
    inv_denom = 1.0 / (float((GRID_HI - GRID_LO) / (GRID_SIZE - 1)) + 1e-06)
    return grid, inv_denom


def silu(v):
    e = np.exp(-np.abs(v))
    return v * np.where(v >= 0.0, 1.0, e) / (1.0 + e)


def setup_inputs():
    s = mx_kscale(IN_F)
    x = bf(np.random.standard_normal((BATCH, SEQ, IN_F)) * s)
    base_w = np.random.standard_normal((OUT_F, IN_F)) / np.sqrt(IN_F) / s
    base_w_words, base_w_scales = pack_weight(np.ascontiguousarray(base_w.T), "e4m3")
    base_b = bf(np.random.standard_normal(OUT_F) * 0.1)
    spline_w = bf(np.random.standard_normal((OUT_F, IN_F, GRID_SIZE)) * 0.64 / np.sqrt(IN_F))
    return {"x": x,
            "base_w_words": base_w_words,
            "base_w_scales": base_w_scales,
            "base_b": base_b,
            "spline_w": spline_w}


def reference(x, base_w_words, base_w_scales, base_b, spline_w):
    grid, inv_denom = _grid_and_inv_denom()
    lead = x.shape[:-1]
    x_flat = f64(x).reshape(-1, IN_F)
    act = silu(x_flat)
    base_out = (mxq(act, 1, "e4m3") @ unpack_weight(base_w_words, base_w_scales, "e4m3")) + f64(base_b)
    basis = np.exp(-(((x_flat[..., None] - grid) * inv_denom) ** 2))
    bq = mxq(basis.reshape(-1, IN_F * GRID_SIZE), 1, "e4m3")
    wq = mxq(f64(spline_w).reshape(OUT_F, IN_F * GRID_SIZE), 1, "e4m3")
    spline_out = bq @ wq.T
    out = base_out + spline_out
    return out.reshape(*lead, OUT_F)

@@ -1,0 +1,433 @@
+from contextlib import ExitStack
+
+import concourse.mybir as mybir
+from concourse.masks import make_identity
+
+F32 = mybir.dt.float32
+BF16 = mybir.dt.bfloat16
+I32 = mybir.dt.int32
+U32 = mybir.dt.uint32
+U8 = mybir.dt.uint8
+FP8X4 = mybir.dt.float8_e4m3fn_x4
+ACT = mybir.ActivationFunctionType
+ALU = mybir.AluOpType
+
+P = 128
+ROWS = 128
+IN_F = 2048
+OUT_F = 2048
+GRID = 4
+KS = IN_F * GRID
+UNITS = OUT_F // P
+PASSES = KS // 512
+RAW_BUFS = 6
+FLOPS = 2 * ROWS * OUT_F * (IN_F + KS)
+
+GRID_PTS = [-2.0, -2.0 + 4.0 / 3.0, -2.0 + 8.0 / 3.0, 2.0]
+INV_DENOM = 1.0 / (4.0 / 3.0 + 1e-06)
+
+
+PAIR_UNTIL = 0
+
+
+def parts_of(u):
+    return 4 if u == 15 else 2
+
+
+def pieces_of(u):
+    return 4 if u >= 14 else (2 if u >= 8 else 1)
+
+
+def vector_banks(u):
+    if u == 0:
+        return (0, 1, 2, 3, 4, 5)
+    if u == 1:
+        return (0,)
+    return (0, 4)
+
+
+def plan():
+    steps = []
+    add = steps.append
+
+    def load_unit(u):
+        for q in range(pieces_of(u)):
+            add(("load_w", u, q, pieces_of(u)))
+
+    def finish_unit(u):
+        for q in range(parts_of(u)):
+            add(("mx", u, q))
+        add(("ev", u))
+
+    add(("consts",))
+    add(("load_x",))
+    add(("load_bias",))
+    for quad in range(4):
+        add(("load_bscale", quad))
+    for g in range(4):
+        add(("load_bw", g))
+    for u in range(3):
+        load_unit(u)
+    add(("warm",))
+    add(("T_silu", 0))
+    add(("T_silu", 1))
+    for m in range(4):
+        add(("dup", m))
+    add(("T_xd", 0))
+    add(("T_xd", 1))
+    add(("mm_bias", 0))
+    add(("mm_bias", 1))
+    for g in range(4):
+        add(("silu", g))
+    add(("q_a",))
+    add(("mx_base", 0))
+    add(("sq", 1, 0, "V"))
+    add(("ev_bias", 0))
+    add(("ev_bias", 1))
+    add(("T_xd", 2))
+    add(("T_xd", 3))
+    add(("sq", 0, 0, "A"))
+    add(("sq", 0, 1, "A"))
+    add(("exp", 0))
+    add(("sq", 1, 1, "V"))
+    add(("q_b", 0))
+    add(("sq", 2, 0, "A"))
+    add(("sq", 2, 1, "A"))
+    add(("exp", 1))
+    add(("sq", 3, 0, "V"))
+    add(("exp", 2))
+    add(("sq", 3, 1, "A"))
+    add(("exp", 3))
+    for g in range(1, 4):
+        add(("mx_base", g))
+    load_unit(3)
+    load_unit(4)
+    for j in range(4):
+        add(("ev_base", j))
+    add(("q_b", 1))
+
+    late_qb = {(0, 0): 2, (0, 1): 3}
+    pend = None
+    owed = []
+    for u in range(15):
+        for q in range(2):
+            for bl in range(4):
+                add(("T", u, q, bl))
+                add(("copy", u, q, bl, "V" if q * 4 + bl in vector_banks(u) else "A"))
+                if bl == 0 and pend is not None:
+                    add(("q_w",) + pend)
+            pend = (u, q)
+            if (u, q) in late_qb:
+                add(("q_b", late_qb[(u, q)]))
+        if u + 5 < 16:
+            load_unit(u + 5)
+        if u > 0:
+            owed.append(u - 1)
+        if u % 2 == 1 or u >= PAIR_UNTIL:
+            if u % 2 == 1 and u < PAIR_UNTIL:
+                owed.append(u)
+            for v in owed:
+                if v not in done_units(steps):
+                    finish_unit(v)
+            owed = []
+        if u == 13:
+            add(("store", 0, 12))
+    add(("q_w",) + pend)
+    for q in range(4):
+        for bl in range(2):
+            add(("T", 15, q, bl))
+            add(("copy", 15, q, bl, "V" if (q, bl) == (3, 0) else "A"))
+        add(("q_w", 15, q))
+    finish_unit(14)
+    add(("store", 12, 15))
+    finish_unit(15)
+    add(("store", 15, 16))
+    return steps
+
+
+def done_units(steps):
+    return [s[1] for s in steps if s[0] == "ev"]
+
+
+def tile_kanlinear_w_kernel(tc, x, base_w_words, base_w_scales, base_b, spline_w, out):
+    nc = tc.nc
+    xf = x.flatten_outer_dims()
+    of = out.flatten_outer_dims()
+    w2 = spline_w.rearrange("o i g -> o (i g)")
+
+    with ExitStack() as ctx:
+        const = ctx.enter_context(tc.tile_pool(name="const", bufs=1))
+        rawp = ctx.enter_context(tc.tile_pool(name="rawp", bufs=RAW_BUFS))
+        grpp = ctx.enter_context(tc.tile_pool(name="grpp", bufs=3))
+        codp = ctx.enter_context(tc.tile_pool(name="codp", bufs=4))
+        zp = ctx.enter_context(tc.tile_pool(name="zp", bufs=2))
+        ps = ctx.enter_context(tc.psum_pool(name="ps", bufs=8))
+        ctx.enter_context(tc.manual_schedule())
+
+        ident_f = const.tile([P, P], F32, name="ident_f")
+        ident_b = const.tile([P, P], BF16, name="ident_b")
+        ones = const.tile([P, P], BF16, name="ones")
+        par = const.tile([P, 1], F32, name="par")
+        nb = const.tile([P, 2], F32, name="nb")
+        warm = const.tile([P, 2], F32, name="warm")
+        brow = const.tile([P, OUT_F], BF16, name="brow")
+        bs = const.tile([P, OUT_F], U8, name="bs", align_bytes=64)
+        acodes = const.tile([P, 4 * ROWS], U32, name="acodes", align_bytes=64)
+        ascales = const.tile([P, 4 * ROWS], U8, name="ascales", align_bytes=64)
+        bcodes = const.tile([P, PASSES * ROWS], U32, name="bcodes", align_bytes=64)
+        bscales = const.tile([P, PASSES * ROWS], U8, name="bscales", align_bytes=64)
+        spl = const.tile([P, OUT_F], F32, name="spl")
+        bias_sb = const.tile([P, OUT_F], BF16, name="bias_sb")
+        xt = rawp.tile([P, KS], BF16, name="xt", tag="raw", align_bytes=64)
+        x_sb = xt[:, 0:IN_F]
+        xdup = xt[:, IN_F : 3 * IN_F]
+        ast = xt[:, 3 * IN_F : 4 * IN_F]
+
+        live = {}
+
+        for step in plan():
+            kind = step[0]
+            if kind == "consts":
+                nc.vector.memset(bs[:].bitcast(I32), 0)
+                nc.vector.memset(brow[:].bitcast(I32), 0)
+                nc.vector.memset(ones[:], 1.0)
+                nc.vector.memset(warm[:], 0.0)
+                make_identity(nc, ident_f[:])
+                make_identity(nc, ident_b[:])
+                nc.vector.tensor_reduce(
+                    out=par[:],
+                    in_=ident_f[:, 0:P:2],
+                    axis=mybir.AxisListType.X,
+                    op=ALU.add,
+                )
+                for e in range(2):
+                    nc.vector.tensor_scalar(
+                        out=nb[:, e : e + 1],
+                        in0=par[:],
+                        scalar1=INV_DENOM * (GRID_PTS[2 + e] - GRID_PTS[e]),
+                        scalar2=-INV_DENOM * GRID_PTS[2 + e],
+                        op0=ALU.mult,
+                        op1=ALU.add,
+                    )
+            elif kind == "load_x":
+                nc.sync.dma_start(out=x_sb, in_=xf)
+            elif kind == "load_bias":
+                nc.scalar.dma_start(out=brow[0:1, :], in_=base_b.rearrange("(o n) -> o n", o=1))
+            elif kind == "load_bscale":
+                quad = step[1]
+                nc.sync.dma_start(
+                    out=bs[32 * quad : 32 * quad + 16, :].bitcast(I32),
+                    in_=base_w_scales[:, 4 * quad : 4 * quad + 4, :].bitcast(I32),
+                )
+            elif kind == "load_bw":
+                g = step[1]
+                if g % 2 == 0:
+                    bw = rawp.tile([P, 2 * OUT_F], I32, name="bw", tag="raw", align_bytes=64)
+                    live[("bw", g // 2)] = bw
+                bw = live[("bw", g // 2)]
+                nc.sync.dma_start(
+                    out=bw[:, OUT_F * (g % 2) : OUT_F * (g % 2 + 1)],
+                    in_=base_w_words[g].rearrange("p n t -> p (n t)").bitcast(I32),
+                )
+            elif kind == "load_w":
+                u, q, nq = step[1], step[2], step[3]
+                if q == 0:
+                    raw = rawp.tile([P, KS], BF16, name="raw", tag="raw", align_bytes=64)
+                    live[("raw", u)] = raw
+                raw = live[("raw", u)]
+                width = KS // nq
+                nc.sync.dma_start(
+                    out=raw[:, width * q : width * (q + 1)],
+                    in_=w2[P * u : P * (u + 1), width * q : width * (q + 1)],
+                )
+            elif kind == "warm":
+                nc.scalar.activation(out=warm[:, 1:2], in_=warm[:, 0:1], func=ACT.Silu)
+            elif kind == "T_silu":
+                gg = step[1]
+                xs = ps.tile([P, 512], F32, name="xs", tag="ps")
+                live[("xs", gg)] = xs
+                xw = x_sb.bitcast(F32)
+                for k in range(4):
+                    g = 2 * gg + k // 2
+                    uu = k % 2
+                    nc.tensor.transpose(
+                        out=xs[:, P * k : P * (k + 1)],
+                        in_=xw[:, 256 * g + uu : 256 * (g + 1) : 2],
+                        identity=ident_f[:],
+                    )
+            elif kind == "silu":
+                g = step[1]
+                xs = live[("xs", g // 2)]
+                half = 256 * (g % 2)
+                nc.scalar.activation(
+                    out=ast[:, 512 * g : 512 * (g + 1)].rearrange("p (r u e) -> p r u e", u=2, e=2),
+                    in_=xs[:, half : half + 256].bitcast(BF16).rearrange("p (u r e) -> p r u e", u=2, e=2),
+                    func=ACT.Silu,
+                )
+            elif kind == "q_a":
+                nc.vector.quantize_mx(out=acodes[:].bitcast(FP8X4), scales=ascales[:], in_=ast)
+            elif kind == "mm_bias":
+                j = step[1]
+                bb = ps.tile([P, 1024], BF16, name="bb", tag="ps")
+                live[("bb", j)] = bb
+                for h in range(2):
+                    nc.tensor.matmul(
+                        out=bb[:, 512 * h : 512 * (h + 1)],
+                        lhsT=ones[:],
+                        rhs=brow[:, 1024 * j + 512 * h : 1024 * j + 512 * (h + 1)],
+                        start=True,
+                        stop=True,
+                    )
+            elif kind == "ev_bias":
+                j = step[1]
+                nc.vector.tensor_copy(out=bias_sb[:, 1024 * j : 1024 * (j + 1)], in_=live[("bb", j)][:])
+            elif kind == "dup":
+                m = step[1]
+                nc.gpsimd.tensor_scalar(
+                    out=xdup[:, 1024 * m : 1024 * (m + 1)].rearrange("p (i b) -> p i b", b=2),
+                    in0=x_sb[:, 512 * m : 512 * (m + 1)].unsqueeze(2).to_broadcast([P, 512, 2]),
+                    scalar1=1.0,
+                    scalar2=0.0,
+                    op0=ALU.mult,
+                    op1=ALU.add,
+                )
+            elif kind == "T_xd":
+                m = step[1]
+                xd = ps.tile([P, 1024], BF16, name="xd", tag="ps")
+                live[("xd", m)] = xd
+                for k in range(8):
+                    nc.tensor.transpose(
+                        out=xd[:, P * k : P * (k + 1)],
+                        in_=xdup[:, 1024 * m + P * k : 1024 * m + P * (k + 1)],
+                        identity=ident_b[:],
+                    )
+            elif kind == "sq":
+                m, e, eng = step[1], step[2], step[3]
+                if ("zt", m) not in live:
+                    zt = zp.tile([P, 2, 1024], F32, name="zt", tag="zt", bufs=4)
+                    live[("zt", m)] = zt
+                zt = live[("zt", m)]
+                zdst = zt[:, e, :].rearrange("p (c r h) -> p c r h", c=4, h=2)
+                xsrc = live[("xd", m)][:].rearrange("p (c h r) -> p c r h", c=4, h=2)
+                if eng == "A":
+                    nc.scalar.activation(out=zdst, in_=xsrc, func=ACT.Square, bias=nb[:, e : e + 1], scale=INV_DENOM)
+                else:
+                    nc.vector.tensor_scalar(
+                        out=zdst,
+                        in0=xsrc,
+                        scalar1=INV_DENOM,
+                        scalar2=nb[:, e : e + 1],
+                        op0=ALU.mult,
+                        op1=ALU.add,
+                    )
+                    nc.vector.tensor_tensor(out=zt[:, e, :], in0=zt[:, e, :], in1=zt[:, e, :], op=ALU.mult)
+            elif kind == "exp":
+                m = step[1]
+                bst = zp.tile([P, 2048], BF16, name="bst", tag="bst", bufs=4, align_bytes=64)
+                live[("bst", m)] = bst
+                nc.scalar.activation(
+                    out=bst[:].rearrange("p (n e) -> p n e", e=2),
+                    in_=live[("zt", m)][:].rearrange("p e n -> p n e"),
+                    func=ACT.Exp,
+                    scale=-1.0,
+                )
+            elif kind == "q_b":
+                m = step[1]
+                nc.vector.quantize_mx(
+                    out=bcodes[:, 512 * m : 512 * (m + 1)].bitcast(FP8X4),
+                    scales=bscales[:, 512 * m : 512 * (m + 1)],
+                    in_=live[("bst", m)][:],
+                )
+            elif kind == "mx_base":
+                g = step[1]
+                for j in range(4):
+                    if g == 0:
+                        bp = ps.tile([P, 512], F32, name="bp", tag="ps")
+                        live[("bp", j)] = bp
+                    nc.tensor.matmul_mx(
+                        out=live[("bp", j)][:],
+                        lhsT=acodes[:, ROWS * g : ROWS * (g + 1)].bitcast(FP8X4),
+                        lhsT_scale=ascales[:, ROWS * g : ROWS * (g + 1)],
+                        rhs=live[("bw", g // 2)][
+                            :, OUT_F * (g % 2) + 512 * j : OUT_F * (g % 2) + 512 * (j + 1)
+                        ].bitcast(FP8X4),
+                        rhs_scale=bs[4 * g : P, 512 * j : 512 * (j + 1)],
+                        start=(g == 0),
+                        stop=(g == 3),
+                    )
+            elif kind == "ev_base":
+                j = step[1]
+                nc.vector.tensor_tensor(
+                    out=spl[:, 512 * j : 512 * (j + 1)],
+                    in0=live[("bp", j)][:],
+                    in1=bias_sb[:, 512 * j : 512 * (j + 1)],
+                    op=ALU.add,
+                )
+            elif kind == "T":
+                u, q, bl = step[1], step[2], step[3]
+                npass = PASSES // parts_of(u)
+                if bl == 0:
+                    if npass == 4:
+                        grp = zp.tile([P, 2048], BF16, name="grp", tag="bst", bufs=4, align_bytes=64)
+                    else:
+                        grp = grpp.tile([P, 4096], BF16, name="grp", tag="grp", align_bytes=64)
+                    live[("grp", u, q)] = grp
+                pt = ps.tile([P, 512], F32, name="pt", tag="ps")
+                live[("pt", u, q, bl)] = pt
+                rawf = live[("raw", u)][:].bitcast(F32)
+                w0 = (npass * q + 2 * bl) * 256
+                for k in range(4):
+                    nc.tensor.transpose(
+                        out=pt[:, P * k : P * (k + 1)],
+                        in_=rawf[:, w0 + P * k : w0 + P * (k + 1)],
+                        identity=ident_f[:],
+                    )
+            elif kind == "copy":
+                u, q, bl, eng = step[1], step[2], step[3], step[4]
+                dst = live[("grp", u, q)][:].bitcast(F32)[:, 512 * bl : 512 * (bl + 1)]
+                dst = dst.rearrange("p (c o h) -> p c o h", c=2, h=2)
+                src = live[("pt", u, q, bl)][:].rearrange("p (c h o) -> p c o h", c=2, h=2)
+                if eng == "V":
+                    nc.vector.tensor_copy(out=dst, in_=src)
+                else:
+                    nc.scalar.copy(out=dst, in_=src)
+            elif kind == "q_w":
+                u, q = step[1], step[2]
+                npass = PASSES // parts_of(u)
+                sfx = "s" if npass == 4 else ""
+                cod = codp.tile([P, npass * P], U32, name="cod", tag="cod" + sfx, align_bytes=64)
+                scl = codp.tile([P, npass * P], U8, name="scl", tag="scl" + sfx, align_bytes=64)
+                live[("cod", u, q)] = cod
+                live[("scl", u, q)] = scl
+                nc.vector.quantize_mx(out=cod[:].bitcast(FP8X4), scales=scl[:], in_=live[("grp", u, q)][:])
+            elif kind == "mx":
+                u, q = step[1], step[2]
+                npass = PASSES // parts_of(u)
+                if q == 0:
+                    acc = ps.tile([P, 512], F32, name="acc", tag="ps")
+                    live[("acc", u)] = acc
+                acc = live[("acc", u)]
+                cod = live[("cod", u, q)]
+                scl = live[("scl", u, q)]
+                for cl in range(npass):
+                    c = npass * q + cl
+                    nc.tensor.matmul_mx(
+                        out=acc[:, 0:P],
+                        lhsT=bcodes[:, ROWS * c : ROWS * (c + 1)].bitcast(FP8X4),
+                        lhsT_scale=bscales[:, ROWS * c : ROWS * (c + 1)],
+                        rhs=cod[:, P * cl : P * (cl + 1)].bitcast(FP8X4),
+                        rhs_scale=scl[:, P * cl : P * (cl + 1)],
+                        start=(c == 0),
+                        stop=(c == PASSES - 1),
+                    )
+            elif kind == "ev":
+                u = step[1]
+                nc.vector.tensor_tensor(
+                    out=spl[:, P * u : P * (u + 1)],
+                    in0=live[("acc", u)][:, 0:P],
+                    in1=spl[:, P * u : P * (u + 1)],
+                    op=ALU.add,
+                )
+            elif kind == "store":
+                lo, hi = step[1], step[2]
+                nc.sync.dma_start(out=of[:, P * lo : P * hi], in_=spl[:, P * lo : P * hi])

@@ -27,9 +27,6 @@ GRID_PTS = [-2.0, -2.0 + 4.0 / 3.0, -2.0 + 8.0 / 3.0, 2.0]
 INV_DENOM = 1.0 / (4.0 / 3.0 + 1e-06)
 
 
-PAIR_UNTIL = 0
-
-
 def parts_of(u):
     return 4 if u == 15 else 2
 
@@ -108,7 +105,6 @@ def plan():
 
     late_qb = {(0, 0): 2, (0, 1): 3}
     pend = None
-    owed = []
     for u in range(15):
         for q in range(2):
             for bl in range(4):
@@ -119,17 +115,14 @@ def plan():
             pend = (u, q)
             if (u, q) in late_qb:
                 add(("q_b", late_qb[(u, q)]))
+            if u > 1 or (u, q) == (1, 1):
+                if (u, q) == (1, 1):
+                    add(("mx", 0, 0))
+                add(("mx", u - 1, q))
+                if q == 1:
+                    add(("ev", u - 1))
         if u + 5 < 16:
             load_unit(u + 5)
-        if u > 0:
-            owed.append(u - 1)
-        if u % 2 == 1 or u >= PAIR_UNTIL:
-            if u % 2 == 1 and u < PAIR_UNTIL:
-                owed.append(u)
-            for v in owed:
-                if v not in done_units(steps):
-                    finish_unit(v)
-            owed = []
         if u == 13:
             add(("store", 0, 12))
     add(("q_w",) + pend)
@@ -143,10 +136,6 @@ def plan():
     finish_unit(15)
     add(("store", 15, 16))
     return steps
-
-
-def done_units(steps):
-    return [s[1] for s in steps if s[0] == "ev"]
 
 
 def tile_kanlinear_w_kernel(tc, x, base_w_words, base_w_scales, base_b, spline_w, out):

@@ -27,12 +27,16 @@ GRID_PTS = [-2.0, -2.0 + 4.0 / 3.0, -2.0 + 8.0 / 3.0, 2.0]
 INV_DENOM = 1.0 / (4.0 / 3.0 + 1e-06)
 
 
+FINE = False
+PIECES_FROM = 12
+
+
 def parts_of(u):
     return 4 if u == 15 else 2
 
 
 def pieces_of(u):
-    return 4 if u >= 14 else (2 if u >= 8 else 1)
+    return 4 if u >= PIECES_FROM else 1
 
 
 def vector_banks(u):
@@ -51,19 +55,14 @@ def plan():
         for q in range(pieces_of(u)):
             add(("load_w", u, q, pieces_of(u)))
 
-    def finish_unit(u):
-        for q in range(parts_of(u)):
-            add(("mx", u, q))
-        add(("ev", u))
-
     add(("consts",))
     add(("load_x",))
     add(("load_bias",))
     for quad in range(4):
         add(("load_bscale", quad))
     for g in range(4):
-        add(("load_bw", g))
-    for u in range(3):
+        add(("load_bw", 0, g, 0, 2))
+    for u in range(4):
         load_unit(u)
     add(("warm",))
     add(("T_silu", 0))
@@ -77,12 +76,13 @@ def plan():
     for g in range(4):
         add(("silu", g))
     add(("q_a",))
-    add(("mx_base", 0))
     add(("sq", 1, 0, "V"))
     add(("ev_bias", 0))
     add(("ev_bias", 1))
     add(("T_xd", 2))
     add(("T_xd", 3))
+    for g in range(4):
+        add(("mx_base", 0, g, 0, 2))
     add(("sq", 0, 0, "A"))
     add(("sq", 0, 1, "A"))
     add(("exp", 0))
@@ -91,16 +91,13 @@ def plan():
     add(("sq", 2, 0, "A"))
     add(("sq", 2, 1, "A"))
     add(("exp", 1))
+    add(("ev_base", 0))
+    add(("ev_base", 1))
+    load_unit(4)
     add(("sq", 3, 0, "V"))
     add(("exp", 2))
     add(("sq", 3, 1, "A"))
     add(("exp", 3))
-    for g in range(1, 4):
-        add(("mx_base", g))
-    load_unit(3)
-    load_unit(4)
-    for j in range(4):
-        add(("ev_base", j))
     add(("q_b", 1))
 
     late_qb = {(0, 0): 2, (0, 1): 3}
@@ -115,26 +112,40 @@ def plan():
             pend = (u, q)
             if (u, q) in late_qb:
                 add(("q_b", late_qb[(u, q)]))
-            if u > 1 or (u, q) == (1, 1):
-                if (u, q) == (1, 1):
-                    add(("mx", 0, 0))
+            if u > 0 and (q == 1 or (FINE and u > 1)):
+                if q == 1 and not (FINE and u > 1):
+                    add(("mx", u - 1, 0))
                 add(("mx", u - 1, q))
                 if q == 1:
                     add(("ev", u - 1))
         if u + 5 < 16:
             load_unit(u + 5)
-        if u == 13:
-            add(("store", 0, 12))
+        if u + 5 == 16:
+            for j in range(2):
+                for g in range(4):
+                    add(("load_bw", 1, g, j, j + 1))
+            add(("store", 0, 8))
     add(("q_w",) + pend)
     for q in range(4):
         for bl in range(2):
             add(("T", 15, q, bl))
             add(("copy", 15, q, bl, "V" if (q, bl) == (3, 0) else "A"))
         add(("q_w", 15, q))
-    finish_unit(14)
-    add(("store", 12, 15))
-    finish_unit(15)
-    add(("store", 15, 16))
+    add(("mx", 14, 0))
+    add(("mx", 14, 1))
+    add(("ev", 14))
+    for q in range(3):
+        add(("mx", 15, q))
+    for g in range(4):
+        add(("mx_base", 1, g, 0, 1))
+    add(("ev_late", 2))
+    add(("store", 8, 12))
+    add(("mx", 15, 3))
+    add(("ev", 15))
+    for g in range(4):
+        add(("mx_base", 1, g, 1, 2))
+    add(("ev_late", 3))
+    add(("store", 12, 16))
     return steps
 
 
@@ -209,14 +220,16 @@ def tile_kanlinear_w_kernel(tc, x, base_w_words, base_w_scales, base_b, spline_w
                     in_=base_w_scales[:, 4 * quad : 4 * quad + 4, :].bitcast(I32),
                 )
             elif kind == "load_bw":
-                g = step[1]
-                if g % 2 == 0:
+                half, g, j0, j1 = step[1], step[2], step[3], step[4]
+                if ("bw", half) not in live:
                     bw = rawp.tile([P, 2 * OUT_F], I32, name="bw", tag="raw", align_bytes=64)
-                    live[("bw", g // 2)] = bw
-                bw = live[("bw", g // 2)]
+                    live[("bw", half)] = bw
+                bw = live[("bw", half)]
                 nc.sync.dma_start(
-                    out=bw[:, OUT_F * (g % 2) : OUT_F * (g % 2 + 1)],
-                    in_=base_w_words[g].rearrange("p n t -> p (n t)").bitcast(I32),
+                    out=bw[:, 1024 * g + 512 * j0 : 1024 * g + 512 * j1],
+                    in_=base_w_words[g][:, 1024 * half + 512 * j0 : 1024 * half + 512 * j1, :]
+                    .rearrange("p n t -> p (n t)")
+                    .bitcast(I32),
                 )
             elif kind == "load_w":
                 u, q, nq = step[1], step[2], step[3]
@@ -328,8 +341,9 @@ def tile_kanlinear_w_kernel(tc, x, base_w_words, base_w_scales, base_b, spline_w
                     in_=live[("bst", m)][:],
                 )
             elif kind == "mx_base":
-                g = step[1]
-                for j in range(4):
+                half, g, j0, j1 = step[1], step[2], step[3], step[4]
+                for jl in range(j0, j1):
+                    j = 2 * half + jl
                     if g == 0:
                         bp = ps.tile([P, 512], F32, name="bp", tag="ps")
                         live[("bp", j)] = bp
@@ -337,9 +351,7 @@ def tile_kanlinear_w_kernel(tc, x, base_w_words, base_w_scales, base_b, spline_w
                         out=live[("bp", j)][:],
                         lhsT=acodes[:, ROWS * g : ROWS * (g + 1)].bitcast(FP8X4),
                         lhsT_scale=ascales[:, ROWS * g : ROWS * (g + 1)],
-                        rhs=live[("bw", g // 2)][
-                            :, OUT_F * (g % 2) + 512 * j : OUT_F * (g % 2) + 512 * (j + 1)
-                        ].bitcast(FP8X4),
+                        rhs=live[("bw", half)][:, 1024 * g + 512 * jl : 1024 * g + 512 * (jl + 1)].bitcast(FP8X4),
                         rhs_scale=bs[4 * g : P, 512 * j : 512 * (j + 1)],
                         start=(g == 0),
                         stop=(g == 3),
@@ -350,6 +362,14 @@ def tile_kanlinear_w_kernel(tc, x, base_w_words, base_w_scales, base_b, spline_w
                     out=spl[:, 512 * j : 512 * (j + 1)],
                     in0=live[("bp", j)][:],
                     in1=bias_sb[:, 512 * j : 512 * (j + 1)],
+                    op=ALU.add,
+                )
+            elif kind == "ev_late":
+                j = step[1]
+                nc.vector.tensor_tensor(
+                    out=spl[:, 512 * j : 512 * (j + 1)],
+                    in0=live[("bp", j)][:],
+                    in1=spl[:, 512 * j : 512 * (j + 1)],
                     op=ALU.add,
                 )
             elif kind == "T":
@@ -414,7 +434,7 @@ def tile_kanlinear_w_kernel(tc, x, base_w_words, base_w_scales, base_b, spline_w
                 nc.vector.tensor_tensor(
                     out=spl[:, P * u : P * (u + 1)],
                     in0=live[("acc", u)][:, 0:P],
-                    in1=spl[:, P * u : P * (u + 1)],
+                    in1=(spl if u < 8 else bias_sb)[:, P * u : P * (u + 1)],
                     op=ALU.add,
                 )
             elif kind == "store":

@@ -27,7 +27,7 @@ GRID_PTS = [-2.0, -2.0 + 4.0 / 3.0, -2.0 + 8.0 / 3.0, 2.0]
 INV_DENOM = 1.0 / (4.0 / 3.0 + 1e-06)
 
 
-FINE = False
+FINE_FROM = 99
 PIECES_FROM = 12
 
 
@@ -36,7 +36,7 @@ def parts_of(u):
 
 
 def pieces_of(u):
-    return 4 if u >= PIECES_FROM else 1
+    return 4 if u >= 14 else (2 if u >= PIECES_FROM else 1)
 
 
 def vector_banks(u):
@@ -58,7 +58,7 @@ def plan():
     add(("consts",))
     add(("load_x",))
     add(("load_bias",))
-    for quad in range(4):
+    for quad in (0, 2, 1, 3):
         add(("load_bscale", quad))
     for g in range(4):
         add(("load_bw", 0, g, 0, 2))
@@ -112,8 +112,9 @@ def plan():
             pend = (u, q)
             if (u, q) in late_qb:
                 add(("q_b", late_qb[(u, q)]))
-            if u > 0 and (q == 1 or (FINE and u > 1)):
-                if q == 1 and not (FINE and u > 1):
+            fine = u > max(1, FINE_FROM)
+            if u > 0 and (q == 1 or fine):
+                if q == 1 and not fine:
                     add(("mx", u - 1, 0))
                 add(("mx", u - 1, q))
                 if q == 1:
@@ -138,14 +139,16 @@ def plan():
         add(("mx", 15, q))
     for g in range(4):
         add(("mx_base", 1, g, 0, 1))
-    add(("ev_late", 2))
+    add(("ev_late", 8, 12))
     add(("store", 8, 12))
     add(("mx", 15, 3))
     add(("ev", 15))
     for g in range(4):
         add(("mx_base", 1, g, 1, 2))
-    add(("ev_late", 3))
-    add(("store", 12, 16))
+    add(("ev_late", 12, 14))
+    add(("store", 12, 14))
+    add(("ev_late", 14, 16))
+    add(("store", 14, 16))
     return steps
 
 
@@ -365,11 +368,12 @@ def tile_kanlinear_w_kernel(tc, x, base_w_words, base_w_scales, base_b, spline_w
                     op=ALU.add,
                 )
             elif kind == "ev_late":
-                j = step[1]
+                lo, hi = step[1], step[2]
+                j = lo // 4
                 nc.vector.tensor_tensor(
-                    out=spl[:, 512 * j : 512 * (j + 1)],
-                    in0=live[("bp", j)][:],
-                    in1=spl[:, 512 * j : 512 * (j + 1)],
+                    out=spl[:, P * lo : P * hi],
+                    in0=live[("bp", j)][:, P * lo - 512 * j : P * hi - 512 * j],
+                    in1=spl[:, P * lo : P * hi],
                     op=ALU.add,
                 )
             elif kind == "T":

@@ -59,7 +59,7 @@ def plan():
     add(("load_x",))
     add(("load_bias",))
     for quad in (0, 2, 1, 3):
-        add(("load_bscale", quad))
+        add(("load_bscale", 0, quad))
     for g in range(4):
         add(("load_bw", 0, g, 0, 2))
     for u in range(4):
@@ -122,6 +122,8 @@ def plan():
         if u + 5 < 16:
             load_unit(u + 5)
         if u + 5 == 16:
+            for quad in (0, 2, 1, 3):
+                add(("load_bscale", 1, quad))
             for j in range(2):
                 for g in range(4):
                     add(("load_bw", 1, g, j, j + 1))
@@ -130,7 +132,7 @@ def plan():
     for q in range(4):
         for bl in range(2):
             add(("T", 15, q, bl))
-            add(("copy", 15, q, bl, "V" if (q, bl) == (3, 0) else "A"))
+            add(("copy", 15, q, bl, "V" if (q, bl) in ((1, 1), (3, 0)) else "A"))
         add(("q_w", 15, q))
     add(("mx", 14, 0))
     add(("mx", 14, 1))
@@ -217,10 +219,10 @@ def tile_kanlinear_w_kernel(tc, x, base_w_words, base_w_scales, base_b, spline_w
             elif kind == "load_bias":
                 nc.scalar.dma_start(out=brow[0:1, :], in_=base_b.rearrange("(o n) -> o n", o=1))
             elif kind == "load_bscale":
-                quad = step[1]
+                cols, quad = slice(1024 * step[1], 1024 * (step[1] + 1)), step[2]
                 nc.sync.dma_start(
-                    out=bs[32 * quad : 32 * quad + 16, :].bitcast(I32),
-                    in_=base_w_scales[:, 4 * quad : 4 * quad + 4, :].bitcast(I32),
+                    out=bs[32 * quad : 32 * quad + 16, cols].bitcast(I32),
+                    in_=base_w_scales[:, 4 * quad : 4 * quad + 4, cols].bitcast(I32),
                 )
             elif kind == "load_bw":
                 half, g, j0, j1 = step[1], step[2], step[3], step[4]

from contextlib import ExitStack

import concourse.mybir as mybir
from concourse.masks import make_identity

F32 = mybir.dt.float32
BF16 = mybir.dt.bfloat16
I32 = mybir.dt.int32
U32 = mybir.dt.uint32
U8 = mybir.dt.uint8
FP8X4 = mybir.dt.float8_e4m3fn_x4
ACT = mybir.ActivationFunctionType
ALU = mybir.AluOpType

P = 128
ROWS = 128
IN_F = 2048
OUT_F = 2048
GRID = 4
KS = IN_F * GRID
UNITS = OUT_F // P
PASSES = KS // 512
RAW_BUFS = 6
FLOPS = 2 * ROWS * OUT_F * (IN_F + KS)

GRID_PTS = [-2.0, -2.0 + 4.0 / 3.0, -2.0 + 8.0 / 3.0, 2.0]
INV_DENOM = 1.0 / (4.0 / 3.0 + 1e-06)


FINE_FROM = 99
PIECES_FROM = 12


def parts_of(u):
    return 4 if u == 15 else 2


def pieces_of(u):
    return 4 if u >= 14 else (2 if u >= PIECES_FROM else 1)


def vector_banks(u):
    if u == 0:
        return (0, 1, 2, 3, 4, 5)
    if u == 1:
        return (0,)
    return (0, 4)


def plan():
    steps = []
    add = steps.append

    def load_unit(u):
        for q in range(pieces_of(u)):
            add(("load_w", u, q, pieces_of(u)))

    add(("consts",))
    add(("load_x",))
    add(("load_bias",))
    for quad in (0, 2, 1, 3):
        add(("load_bscale", 0, quad))
    for g in range(4):
        add(("load_bw", 0, g, 0, 2))
    for u in range(4):
        load_unit(u)
    add(("warm",))
    add(("T_silu", 0))
    add(("T_silu", 1))
    for m in range(4):
        add(("dup", m))
    add(("T_xd", 0))
    add(("T_xd", 1))
    add(("mm_bias", 0))
    add(("mm_bias", 1))
    for g in range(4):
        add(("silu", g))
    add(("q_a",))
    add(("sq", 1, 0, "V"))
    add(("ev_bias", 0))
    add(("ev_bias", 1))
    add(("T_xd", 2))
    add(("T_xd", 3))
    for g in range(4):
        add(("mx_base", 0, g, 0, 2))
    add(("sq", 0, 0, "A"))
    add(("sq", 0, 1, "A"))
    add(("exp", 0))
    add(("sq", 1, 1, "V"))
    add(("q_b", 0))
    add(("sq", 2, 0, "A"))
    add(("sq", 2, 1, "A"))
    add(("exp", 1))
    add(("ev_base", 0))
    add(("ev_base", 1))
    load_unit(4)
    add(("sq", 3, 0, "V"))
    add(("exp", 2))
    add(("sq", 3, 1, "A"))
    add(("exp", 3))
    add(("q_b", 1))

    late_qb = {(0, 0): 2, (0, 1): 3}
    pend = None
    for u in range(15):
        for q in range(2):
            for bl in range(4):
                add(("T", u, q, bl))
                add(("copy", u, q, bl, "V" if q * 4 + bl in vector_banks(u) else "A"))
                if bl == 0 and pend is not None:
                    add(("q_w",) + pend)
            pend = (u, q)
            if (u, q) in late_qb:
                add(("q_b", late_qb[(u, q)]))
            fine = u > max(1, FINE_FROM)
            if u > 0 and (q == 1 or fine):
                if q == 1 and not fine:
                    add(("mx", u - 1, 0))
                add(("mx", u - 1, q))
                if q == 1:
                    add(("ev", u - 1))
        if u + 5 < 16:
            load_unit(u + 5)
        if u + 5 == 16:
            for quad in (0, 2, 1, 3):
                add(("load_bscale", 1, quad))
            for j in range(2):
                for g in range(4):
                    add(("load_bw", 1, g, j, j + 1))
            add(("store", 0, 8))
    add(("q_w",) + pend)
    for q in range(4):
        for bl in range(2):
            add(("T", 15, q, bl))
            add(("copy", 15, q, bl, "V" if (q, bl) in ((1, 1), (3, 0)) else "A"))
        add(("q_w", 15, q))
    add(("mx", 14, 0))
    add(("mx", 14, 1))
    add(("ev", 14))
    for q in range(3):
        add(("mx", 15, q))
    for g in range(4):
        add(("mx_base", 1, g, 0, 1))
    add(("ev_late", 8, 12))
    add(("store", 8, 12))
    add(("mx", 15, 3))
    add(("ev", 15))
    for g in range(4):
        add(("mx_base", 1, g, 1, 2))
    add(("ev_late", 12, 14))
    add(("store", 12, 14))
    add(("ev_late", 14, 16))
    add(("store", 14, 16))
    return steps


def tile_kanlinear_w_kernel(tc, x, base_w_words, base_w_scales, base_b, spline_w, out):
    nc = tc.nc
    xf = x.flatten_outer_dims()
    of = out.flatten_outer_dims()
    w2 = spline_w.rearrange("o i g -> o (i g)")

    with ExitStack() as ctx:
        const = ctx.enter_context(tc.tile_pool(name="const", bufs=1))
        rawp = ctx.enter_context(tc.tile_pool(name="rawp", bufs=RAW_BUFS))
        grpp = ctx.enter_context(tc.tile_pool(name="grpp", bufs=3))
        codp = ctx.enter_context(tc.tile_pool(name="codp", bufs=4))
        zp = ctx.enter_context(tc.tile_pool(name="zp", bufs=2))
        ps = ctx.enter_context(tc.psum_pool(name="ps", bufs=8))
        ctx.enter_context(tc.manual_schedule())

        ident_f = const.tile([P, P], F32, name="ident_f")
        ident_b = const.tile([P, P], BF16, name="ident_b")
        ones = const.tile([P, P], BF16, name="ones")
        par = const.tile([P, 1], F32, name="par")
        nb = const.tile([P, 2], F32, name="nb")
        warm = const.tile([P, 2], F32, name="warm")
        brow = const.tile([P, OUT_F], BF16, name="brow")
        bs = const.tile([P, OUT_F], U8, name="bs", align_bytes=64)
        acodes = const.tile([P, 4 * ROWS], U32, name="acodes", align_bytes=64)
        ascales = const.tile([P, 4 * ROWS], U8, name="ascales", align_bytes=64)
        bcodes = const.tile([P, PASSES * ROWS], U32, name="bcodes", align_bytes=64)
        bscales = const.tile([P, PASSES * ROWS], U8, name="bscales", align_bytes=64)
        spl = const.tile([P, OUT_F], F32, name="spl")
        bias_sb = const.tile([P, OUT_F], BF16, name="bias_sb")
        xt = rawp.tile([P, KS], BF16, name="xt", tag="raw", align_bytes=64)
        x_sb = xt[:, 0:IN_F]
        xdup = xt[:, IN_F : 3 * IN_F]
        ast = xt[:, 3 * IN_F : 4 * IN_F]

        live = {}

        for step in plan():
            kind = step[0]
            if kind == "consts":
                nc.vector.memset(bs[:].bitcast(I32), 0)
                nc.vector.memset(brow[:].bitcast(I32), 0)
                nc.vector.memset(ones[:], 1.0)
                nc.vector.memset(warm[:], 0.0)
                make_identity(nc, ident_f[:])
                make_identity(nc, ident_b[:])
                nc.vector.tensor_reduce(
                    out=par[:],
                    in_=ident_f[:, 0:P:2],
                    axis=mybir.AxisListType.X,
                    op=ALU.add,
                )
                for e in range(2):
                    nc.vector.tensor_scalar(
                        out=nb[:, e : e + 1],
                        in0=par[:],
                        scalar1=INV_DENOM * (GRID_PTS[2 + e] - GRID_PTS[e]),
                        scalar2=-INV_DENOM * GRID_PTS[2 + e],
                        op0=ALU.mult,
                        op1=ALU.add,
                    )
            elif kind == "load_x":
                nc.sync.dma_start(out=x_sb, in_=xf)
            elif kind == "load_bias":
                nc.scalar.dma_start(out=brow[0:1, :], in_=base_b.rearrange("(o n) -> o n", o=1))
            elif kind == "load_bscale":
                cols, quad = slice(1024 * step[1], 1024 * (step[1] + 1)), step[2]
                nc.sync.dma_start(
                    out=bs[32 * quad : 32 * quad + 16, cols].bitcast(I32),
                    in_=base_w_scales[:, 4 * quad : 4 * quad + 4, cols].bitcast(I32),
                )
            elif kind == "load_bw":
                half, g, j0, j1 = step[1], step[2], step[3], step[4]
                if ("bw", half) not in live:
                    bw = rawp.tile([P, 2 * OUT_F], I32, name="bw", tag="raw", align_bytes=64)
                    live[("bw", half)] = bw
                bw = live[("bw", half)]
                nc.sync.dma_start(
                    out=bw[:, 1024 * g + 512 * j0 : 1024 * g + 512 * j1],
                    in_=base_w_words[g][:, 1024 * half + 512 * j0 : 1024 * half + 512 * j1, :]
                    .rearrange("p n t -> p (n t)")
                    .bitcast(I32),
                )
            elif kind == "load_w":
                u, q, nq = step[1], step[2], step[3]
                if q == 0:
                    raw = rawp.tile([P, KS], BF16, name="raw", tag="raw", align_bytes=64)
                    live[("raw", u)] = raw
                raw = live[("raw", u)]
                width = KS // nq
                nc.sync.dma_start(
                    out=raw[:, width * q : width * (q + 1)],
                    in_=w2[P * u : P * (u + 1), width * q : width * (q + 1)],
                )
            elif kind == "warm":
                nc.scalar.activation(out=warm[:, 1:2], in_=warm[:, 0:1], func=ACT.Silu)
            elif kind == "T_silu":
                gg = step[1]
                xs = ps.tile([P, 512], F32, name="xs", tag="ps")
                live[("xs", gg)] = xs
                xw = x_sb.bitcast(F32)
                for k in range(4):
                    g = 2 * gg + k // 2
                    uu = k % 2
                    nc.tensor.transpose(
                        out=xs[:, P * k : P * (k + 1)],
                        in_=xw[:, 256 * g + uu : 256 * (g + 1) : 2],
                        identity=ident_f[:],
                    )
            elif kind == "silu":
                g = step[1]
                xs = live[("xs", g // 2)]
                half = 256 * (g % 2)
                nc.scalar.activation(
                    out=ast[:, 512 * g : 512 * (g + 1)].rearrange("p (r u e) -> p r u e", u=2, e=2),
                    in_=xs[:, half : half + 256].bitcast(BF16).rearrange("p (u r e) -> p r u e", u=2, e=2),
                    func=ACT.Silu,
                )
            elif kind == "q_a":
                nc.vector.quantize_mx(out=acodes[:].bitcast(FP8X4), scales=ascales[:], in_=ast)
            elif kind == "mm_bias":
                j = step[1]
                bb = ps.tile([P, 1024], BF16, name="bb", tag="ps")
                live[("bb", j)] = bb
                for h in range(2):
                    nc.tensor.matmul(
                        out=bb[:, 512 * h : 512 * (h + 1)],
                        lhsT=ones[:],
                        rhs=brow[:, 1024 * j + 512 * h : 1024 * j + 512 * (h + 1)],
                        start=True,
                        stop=True,
                    )
            elif kind == "ev_bias":
                j = step[1]
                nc.vector.tensor_copy(out=bias_sb[:, 1024 * j : 1024 * (j + 1)], in_=live[("bb", j)][:])
            elif kind == "dup":
                m = step[1]
                nc.gpsimd.tensor_scalar(
                    out=xdup[:, 1024 * m : 1024 * (m + 1)].rearrange("p (i b) -> p i b", b=2),
                    in0=x_sb[:, 512 * m : 512 * (m + 1)].unsqueeze(2).to_broadcast([P, 512, 2]),
                    scalar1=1.0,
                    scalar2=0.0,
                    op0=ALU.mult,
                    op1=ALU.add,
                )
            elif kind == "T_xd":
                m = step[1]
                xd = ps.tile([P, 1024], BF16, name="xd", tag="ps")
                live[("xd", m)] = xd
                for k in range(8):
                    nc.tensor.transpose(
                        out=xd[:, P * k : P * (k + 1)],
                        in_=xdup[:, 1024 * m + P * k : 1024 * m + P * (k + 1)],
                        identity=ident_b[:],
                    )
            elif kind == "sq":
                m, e, eng = step[1], step[2], step[3]
                if ("zt", m) not in live:
                    zt = zp.tile([P, 2, 1024], F32, name="zt", tag="zt", bufs=4)
                    live[("zt", m)] = zt
                zt = live[("zt", m)]
                zdst = zt[:, e, :].rearrange("p (c r h) -> p c r h", c=4, h=2)
                xsrc = live[("xd", m)][:].rearrange("p (c h r) -> p c r h", c=4, h=2)
                if eng == "A":
                    nc.scalar.activation(out=zdst, in_=xsrc, func=ACT.Square, bias=nb[:, e : e + 1], scale=INV_DENOM)
                else:
                    nc.vector.tensor_scalar(
                        out=zdst,
                        in0=xsrc,
                        scalar1=INV_DENOM,
                        scalar2=nb[:, e : e + 1],
                        op0=ALU.mult,
                        op1=ALU.add,
                    )
                    nc.vector.tensor_tensor(out=zt[:, e, :], in0=zt[:, e, :], in1=zt[:, e, :], op=ALU.mult)
            elif kind == "exp":
                m = step[1]
                bst = zp.tile([P, 2048], BF16, name="bst", tag="bst", bufs=4, align_bytes=64)
                live[("bst", m)] = bst
                nc.scalar.activation(
                    out=bst[:].rearrange("p (n e) -> p n e", e=2),
                    in_=live[("zt", m)][:].rearrange("p e n -> p n e"),
                    func=ACT.Exp,
                    scale=-1.0,
                )
            elif kind == "q_b":
                m = step[1]
                nc.vector.quantize_mx(
                    out=bcodes[:, 512 * m : 512 * (m + 1)].bitcast(FP8X4),
                    scales=bscales[:, 512 * m : 512 * (m + 1)],
                    in_=live[("bst", m)][:],
                )
            elif kind == "mx_base":
                half, g, j0, j1 = step[1], step[2], step[3], step[4]
                for jl in range(j0, j1):
                    j = 2 * half + jl
                    if g == 0:
                        bp = ps.tile([P, 512], F32, name="bp", tag="ps")
                        live[("bp", j)] = bp
                    nc.tensor.matmul_mx(
                        out=live[("bp", j)][:],
                        lhsT=acodes[:, ROWS * g : ROWS * (g + 1)].bitcast(FP8X4),
                        lhsT_scale=ascales[:, ROWS * g : ROWS * (g + 1)],
                        rhs=live[("bw", half)][:, 1024 * g + 512 * jl : 1024 * g + 512 * (jl + 1)].bitcast(FP8X4),
                        rhs_scale=bs[4 * g : P, 512 * j : 512 * (j + 1)],
                        start=(g == 0),
                        stop=(g == 3),
                    )
            elif kind == "ev_base":
                j = step[1]
                nc.vector.tensor_tensor(
                    out=spl[:, 512 * j : 512 * (j + 1)],
                    in0=live[("bp", j)][:],
                    in1=bias_sb[:, 512 * j : 512 * (j + 1)],
                    op=ALU.add,
                )
            elif kind == "ev_late":
                lo, hi = step[1], step[2]
                j = lo // 4
                nc.vector.tensor_tensor(
                    out=spl[:, P * lo : P * hi],
                    in0=live[("bp", j)][:, P * lo - 512 * j : P * hi - 512 * j],
                    in1=spl[:, P * lo : P * hi],
                    op=ALU.add,
                )
            elif kind == "T":
                u, q, bl = step[1], step[2], step[3]
                npass = PASSES // parts_of(u)
                if bl == 0:
                    if npass == 4:
                        grp = zp.tile([P, 2048], BF16, name="grp", tag="bst", bufs=4, align_bytes=64)
                    else:
                        grp = grpp.tile([P, 4096], BF16, name="grp", tag="grp", align_bytes=64)
                    live[("grp", u, q)] = grp
                pt = ps.tile([P, 512], F32, name="pt", tag="ps")
                live[("pt", u, q, bl)] = pt
                rawf = live[("raw", u)][:].bitcast(F32)
                w0 = (npass * q + 2 * bl) * 256
                for k in range(4):
                    nc.tensor.transpose(
                        out=pt[:, P * k : P * (k + 1)],
                        in_=rawf[:, w0 + P * k : w0 + P * (k + 1)],
                        identity=ident_f[:],
                    )
            elif kind == "copy":
                u, q, bl, eng = step[1], step[2], step[3], step[4]
                dst = live[("grp", u, q)][:].bitcast(F32)[:, 512 * bl : 512 * (bl + 1)]
                dst = dst.rearrange("p (c o h) -> p c o h", c=2, h=2)
                src = live[("pt", u, q, bl)][:].rearrange("p (c h o) -> p c o h", c=2, h=2)
                if eng == "V":
                    nc.vector.tensor_copy(out=dst, in_=src)
                else:
                    nc.scalar.copy(out=dst, in_=src)
            elif kind == "q_w":
                u, q = step[1], step[2]
                npass = PASSES // parts_of(u)
                sfx = "s" if npass == 4 else ""
                cod = codp.tile([P, npass * P], U32, name="cod", tag="cod" + sfx, align_bytes=64)
                scl = codp.tile([P, npass * P], U8, name="scl", tag="scl" + sfx, align_bytes=64)
                live[("cod", u, q)] = cod
                live[("scl", u, q)] = scl
                nc.vector.quantize_mx(out=cod[:].bitcast(FP8X4), scales=scl[:], in_=live[("grp", u, q)][:])
            elif kind == "mx":
                u, q = step[1], step[2]
                npass = PASSES // parts_of(u)
                if q == 0:
                    acc = ps.tile([P, 512], F32, name="acc", tag="ps")
                    live[("acc", u)] = acc
                acc = live[("acc", u)]
                cod = live[("cod", u, q)]
                scl = live[("scl", u, q)]
                for cl in range(npass):
                    c = npass * q + cl
                    nc.tensor.matmul_mx(
                        out=acc[:, 0:P],
                        lhsT=bcodes[:, ROWS * c : ROWS * (c + 1)].bitcast(FP8X4),
                        lhsT_scale=bscales[:, ROWS * c : ROWS * (c + 1)],
                        rhs=cod[:, P * cl : P * (cl + 1)].bitcast(FP8X4),
                        rhs_scale=scl[:, P * cl : P * (cl + 1)],
                        start=(c == 0),
                        stop=(c == PASSES - 1),
                    )
            elif kind == "ev":
                u = step[1]
                nc.vector.tensor_tensor(
                    out=spl[:, P * u : P * (u + 1)],
                    in0=live[("acc", u)][:, 0:P],
                    in1=(spl if u < 8 else bias_sb)[:, P * u : P * (u + 1)],
                    op=ALU.add,
                )
            elif kind == "store":
                lo, hi = step[1], step[2]
                nc.sync.dma_start(out=of[:, P * lo : P * hi], in_=spl[:, P * lo : P * hi])
